import numpy as np
import ml_dtypes


def mxq(x, axis, fmt="e4m3"):
    dtype, down = {"e4m3": (ml_dtypes.float8_e4m3fn, 7), "e5m2": (ml_dtypes.float8_e5m2, 14)}[fmt]
    v = np.moveaxis(np.asarray(x, np.float32).astype(ml_dtypes.bfloat16).astype(np.float64), axis, -1)
    blocks = v.reshape(v.shape[:-1] + (-1, 32))
    amax = np.abs(blocks).max(-1, keepdims=True)
    byte = np.maximum(np.where(amax > 0, np.frexp(amax)[1] - 1 + 127, 0) - down, 1)
    scale = np.exp2(byte - 127.0)
    codes = (blocks / scale).astype(np.float32).astype(dtype).astype(np.float64)
    return np.moveaxis((codes * scale).reshape(v.shape), -1, axis)


WIDE = False


def mx_kscale(k):
    if not WIDE:
        return np.ones(k)
    levels = np.array([30, -30])
    if k % 512:
        return np.exp2(np.random.permutation(np.resize(levels, k // 32))).repeat(32)
    a = np.empty((k // 512, 16))
    for p in range(k // 512):
        a[p, :8] = np.random.permutation(np.resize(levels, 8))
        for g in range(8):
            far = levels[np.abs(levels - a[p, g]) >= 10]
            a[p, g + 8] = far[np.random.randint(len(far))]
    return np.exp2(a.ravel()).repeat(32)


BF16 = ml_dtypes.bfloat16


def bf(x):
    return np.asarray(x, np.float32).astype(BF16)


def f64(x):
    return np.asarray(x).astype(np.float64)


E2M1 = np.array([0.0, 0.5, 1.0, 1.5, 2.0, 3.0, 4.0, 6.0, -0.0, -0.5, -1.0, -1.5, -2.0, -3.0, -4.0, -6.0])


def pack_weight(w, fmt):
    k, n = w.shape
    w = f64(bf(w)).reshape(k // 32, 32, n)
    amax = np.abs(w).max(1)
    if fmt == "e4m3":
        byte = np.frexp(amax)[1] - 1 + 127 - 7
    else:
        mant, ex = np.frexp(amax / 6.0)
        byte = np.where(mant > 0.5, ex, ex - 1) + 127
    byte = np.clip(np.where(amax > 0, byte, 1), 1, 254)
    scaled = (w * np.exp2(127.0 - byte)[:, None, :]).reshape(k, n).astype(np.float32)
    by_word = np.ascontiguousarray(scaled.reshape(k // 512, 128, 4, n).transpose(0, 1, 3, 2))
    if fmt == "e4m3":
        words = by_word.astype(ml_dtypes.float8_e4m3fn).view(np.uint8)
    else:
        c = by_word.astype(ml_dtypes.float4_e2m1fn).view(np.uint8) & 0xF
        words = c[..., 0::2] | (c[..., 1::2] << 4)
    return np.ascontiguousarray(words), np.ascontiguousarray(byte.astype(np.uint8).reshape(k // 512, 16, n))


def unpack_weight(words, scales, fmt):
    g, p, n, _ = words.shape
    if fmt == "e4m3":
        vals = np.ascontiguousarray(words).view(ml_dtypes.float8_e4m3fn).astype(np.float64)
    else:
        nib = np.empty((g, p, n, 4), np.uint8)
        nib[..., 0::2] = words & 0xF
        nib[..., 1::2] = words >> 4
        vals = E2M1[nib]
    vals = vals * np.repeat(np.exp2(scales.astype(np.float64) - 127.0), 8, axis=1)[..., None]
    return vals.transpose(0, 1, 3, 2).reshape(g * 512, n)

def pack4(w):
    words, scales = pack_weight(w, "e2m1")
    return words.reshape(words.shape[0], 128, -1), scales


def unpack4(words, scales):
    return unpack_weight(words.reshape(words.shape[0], 128, -1, 2), scales, "e2m1")


B, N, C = 2, 512, 1024
R = B * N
G = 3 * C


def sigmoid(v):
    return 1.0 / (1.0 + np.exp(-v))


def setup_inputs():
    s = mx_kscale(C)
    s = s / s.max()
    x_proj = bf(np.random.standard_normal((R, G)))
    annotations = bf(np.random.standard_normal((B, N, C)) * s)
    words, scales = pack4(np.random.standard_normal((C, G)) / np.sqrt(C) / s[:, None])
    bias_h = bf(np.random.standard_normal(G) * 0.3)
    return {"x_proj": x_proj,
            "annotations": annotations,
            "recurrent_kernel_words": words,
            "recurrent_kernel_scales": scales,
            "bias_h": bias_h}


def reference(x_proj, annotations, recurrent_kernel_words, recurrent_kernel_scales, bias_h):
    b, n, c = annotations.shape
    h = f64(annotations).reshape(-1, c)
    mh = (mxq(h, 1, "e5m2") @ unpack4(recurrent_kernel_words, recurrent_kernel_scales)) + f64(bias_h)
    xz, xr, xh = np.split(f64(x_proj), 3, axis=-1)
    hz, hr, hh_in = np.split(mh, 3, axis=-1)
    z = sigmoid(xz + hz)
    r = sigmoid(xr + hr)
    hh = np.tanh(xh + r * hh_in)
    out = z * h + (1.0 - z) * hh
    return out.reshape(b, n, c)

@@ -1,0 +1,273 @@
+from contextlib import ExitStack
+
+import concourse.mybir as mybir
+from concourse.masks import make_identity
+
+F32 = mybir.dt.float32
+BF16 = mybir.dt.bfloat16
+I32 = mybir.dt.int32
+U32 = mybir.dt.uint32
+U8 = mybir.dt.uint8
+E5M2X4 = mybir.dt.float8_e5m2_x4
+E2M1X4 = mybir.dt.float4_e2m1fn_x4
+ACT = mybir.ActivationFunctionType
+ALU = mybir.AluOpType
+
+P = 128
+GRAPHS = 2
+NODES = 512
+C = 1024
+PASSES = 2
+K_PASS = 512
+NODE_TILES = NODES // P
+CH_TILES = C // P
+CHUNK = 512
+UNITS = GRAPHS * CH_TILES
+Z, R, CAND = 0, 1, 2
+FLOPS = 2 * GRAPHS * NODES * C * 3 * C
+
+
+def tile_gatedgraphconvolution_pb_kernel(tc, x_proj, annotations, w_words, w_scales, bias_h, out):
+    nc = tc.nc
+    with ExitStack() as ctx:
+        keep = ctx.enter_context(tc.tile_pool(name="keep", bufs=1))
+        work = ctx.enter_context(tc.tile_pool(name="work", bufs=3))
+        psum = ctx.enter_context(tc.psum_pool(name="psum", bufs=1))
+        ctx.enter_context(tc.manual_schedule())
+
+        ident_f32 = keep.tile([P, P], F32, name="ident_f32")
+        ident_bf16 = keep.tile([P, P], BF16, name="ident_bf16")
+        bias_rows = keep.tile([P, P], BF16, name="bias_rows")
+        bias = keep.tile([P, 3 * CH_TILES], F32, name="bias")
+        scale_plane = keep.tile([P, PASSES, 3 * C], U8, name="scale_plane", align_bytes=64)
+        h_sb, h_codes, h_scales, w_sb, x_sb = {}, {}, {}, {}, {}
+        for gr in range(GRAPHS):
+            for g in range(PASSES):
+                h_sb[gr, g] = keep.tile([P, NODE_TILES, K_PASS], BF16, name="h_%d_%d" % (gr, g))
+                h_codes[gr, g] = keep.tile([P, NODES], U32, name="hc_%d_%d" % (gr, g), align_bytes=64)
+                h_scales[gr, g] = keep.tile([P, NODES], U8, name="hs_%d_%d" % (gr, g), align_bytes=64)
+        for gate in range(3):
+            for ck in range(C // CHUNK):
+                w_sb[gate, ck] = keep.tile([P, PASSES, 2 * CHUNK], U8, name="w_%d_%d" % (gate, ck), align_bytes=64)
+                for gr in range(GRAPHS):
+                    x_sb[gr, gate, ck] = keep.tile([P, NODE_TILES, CHUNK], BF16, name="x_%d_%d_%d" % (gr, gate, ck))
+
+        def load_h(gr, g, t0, t1):
+            src = annotations[gr].rearrange("(t p) k -> p t k", p=P)
+            nc.sync.dma_start(out=h_sb[gr, g][:, t0:t1, :], in_=src[:, t0:t1, g * K_PASS : (g + 1) * K_PASS])
+
+        def load_w(gate, ck):
+            c0 = 2 * (gate * C + ck * CHUNK)
+            src = w_words[:, :, c0 : c0 + 2 * CHUNK].rearrange("g p b -> p g b")
+            nc.sync.dma_start(out=w_sb[gate, ck][:].bitcast(I32), in_=src.bitcast(I32))
+
+        def load_x(gr, gate, ck):
+            c0 = gate * C + ck * CHUNK
+            src = x_proj[gr * NODES : (gr + 1) * NODES, c0 : c0 + CHUNK].rearrange("(t p) c -> p t c", p=P)
+            nc.sync.dma_start(out=x_sb[gr, gate, ck][:], in_=src)
+
+        make_identity(nc, ident_f32[:])
+        nc.gpsimd.memset(bias_rows[:], 0.0)
+        make_identity(nc, ident_bf16[:])
+        nc.scalar.dma_start(out=bias_rows[0 : 3 * CH_TILES, :], in_=bias_h.rearrange("(r c) -> r c", c=P))
+
+        for g in range(PASSES):
+            load_h(0, g, 0, 2)
+            load_h(0, g, 2, 4)
+        for q in range(4):
+            nc.sync.dma_start(
+                out=scale_plane[32 * q : 32 * q + 4, :, :].bitcast(I32),
+                in_=w_scales[:, 4 * q : 4 * q + 4, :].rearrange("g r n -> r g n").bitcast(I32),
+            )
+        load_w(Z, 0)
+        load_w(R, 0)
+        load_x(0, R, 0)
+        load_x(0, Z, 0)
+        load_w(CAND, 0)
+        load_x(0, CAND, 0)
+        for g in range(PASSES):
+            load_h(1, g, 0, 4)
+        for gate in (Z, R, CAND):
+            load_w(gate, 1)
+        for gr, ck in ((0, 1), (1, 0), (1, 1)):
+            for gate in (R, Z, CAND):
+                load_x(gr, gate, ck)
+
+        live = {}
+
+        def h_transpose(piece, tag, bufs):
+            gr, g, half = piece
+            bank = psum.tile([P, 2, 2, P], F32, tag=tag, bufs=bufs, name="ht_bank")
+            for a in range(2):
+                words = h_sb[gr, g][:, 2 * half + a, :].bitcast(F32)
+                for u in range(2):
+                    nc.tensor.transpose(bank[:, a, u, :], words[:, u : 2 * P : 2], ident_f32[:])
+            live["ht", piece] = bank
+
+        def h_copy(piece):
+            grouped = work.tile([P, 2 * P * 4], BF16, name="grouped", align_bytes=64)
+            nc.scalar.copy(
+                out=grouped[:].bitcast(F32).rearrange("p (a r u) -> p a r u", a=2, u=2),
+                in_=live["ht", piece][:].rearrange("p a u r -> p a r u"),
+            )
+            live["grouped", piece] = grouped
+
+        def h_quantize(piece):
+            gr, g, half = piece
+            cols = slice(half * 2 * P, (half + 1) * 2 * P)
+            nc.vector.quantize_mx(
+                out=h_codes[gr, g][:, cols].bitcast(E5M2X4),
+                scales=h_scales[gr, g][:, cols],
+                in_=live["grouped", piece][:],
+            )
+
+        def x_view(k, gate):
+            gr, j = divmod(k, CH_TILES)
+            ck, jj = divmod(j, CHUNK // P)
+            return x_sb[gr, gate, ck][:, :, jj * P : (jj + 1) * P]
+
+        def bias_col(k, gate):
+            col = gate * CH_TILES + k % CH_TILES
+            return bias[:, col : col + 1]
+
+        def recurrent(k, gate, tag):
+            gr, j = divmod(k, CH_TILES)
+            ck, jj = divmod(j, CHUNK // P)
+            bank = psum.tile([P, NODES], F32, tag=tag, name="mx_bank")
+            c0 = gate * C + j * P
+            for g in range(PASSES):
+                nc.tensor.matmul_mx(
+                    out=bank[:],
+                    lhsT=w_sb[gate, ck][:, g, 2 * jj * P : 2 * (jj + 1) * P].bitcast(E2M1X4),
+                    lhsT_scale=scale_plane[:, g, c0 : c0 + P],
+                    rhs=h_codes[gr, g][:].bitcast(E5M2X4),
+                    rhs_scale=h_scales[gr, g][:],
+                    start=(g == 0),
+                    stop=(g == PASSES - 1),
+                )
+            live[tag, k] = bank
+
+        def fresh(name, k, dtype=F32):
+            t = work.tile([P, NODES], dtype, tag=name, name=name)
+            live[name, k] = t
+            return t
+
+        def z_evacuate(k):
+            nc.scalar.activation(out=fresh("mz", k)[:], in_=live["z", k][:], func=ACT.Identity, bias=bias_col(k, Z))
+
+        def z_turn(k):
+            bank = psum.tile([P, NODE_TILES, P], F32, tag="fz", bufs=2, name="fz_bank")
+            mz = live["mz", k]
+            nc.tensor.matmul(out=bank[:], lhsT=ident_bf16[:], rhs=x_view(k, Z), start=True, stop=False)
+            for t in range(NODE_TILES):
+                nc.tensor.matmul(
+                    out=bank[:, t, :], lhsT=mz[:, t * P : (t + 1) * P], rhs=ident_f32[:],
+                    start=False, stop=(t == NODE_TILES - 1), is_transpose=True,
+                )
+            live["fz", k] = bank
+
+        def z_sigmoid(k):
+            src = live["fz", k][:].rearrange("p t c -> p (t c)")
+            nc.scalar.activation(out=fresh("zg", k)[:], in_=src, func=ACT.Sigmoid)
+
+        def xr_turn(k):
+            bank = psum.tile([P, NODES], BF16, tag="xt", name="xt_bank")
+            xr = x_view(k, R)
+            for t in range(NODE_TILES):
+                nc.tensor.transpose(bank[:, t * P : (t + 1) * P], xr[:, t, :], ident_bf16[:])
+            live["xt", k] = bank
+
+        def xr_copy(k):
+            nc.scalar.copy(out=fresh("xrt", k, BF16)[:], in_=live["xt", k][:])
+
+        def r_add(k):
+            nc.vector.tensor_tensor(out=fresh("ar", k)[:], in0=live["r", k][:], in1=live["xrt", k][:], op=ALU.add)
+
+        def r_sigmoid(k):
+            nc.scalar.activation(out=fresh("rg", k)[:], in_=live["ar", k][:], func=ACT.Sigmoid, bias=bias_col(k, R))
+
+        def reset_product(k):
+            nc.vector.scalar_tensor_tensor(
+                out=fresh("rc", k)[:], in0=live["c", k][:], scalar=bias_col(k, CAND), in1=live["rg", k][:],
+                op0=ALU.add, op1=ALU.mult,
+            )
+
+        def cand_turn(k):
+            bank = psum.tile([P, NODE_TILES, P], F32, tag="fh", bufs=1, name="fh_bank")
+            rc = live["rc", k]
+            for t in range(NODE_TILES):
+                nc.tensor.matmul(
+                    out=bank[:, t, :], lhsT=rc[:, t * P : (t + 1) * P], rhs=ident_f32[:],
+                    start=(t == 0), stop=False, is_transpose=True,
+                )
+            nc.tensor.matmul(out=bank[:], lhsT=ident_bf16[:], rhs=x_view(k, CAND), start=False, stop=True)
+            live["fh", k] = bank
+
+        def cand_tanh(k):
+            src = live["fh", k][:].rearrange("p t c -> p (t c)")
+            nc.scalar.activation(out=fresh("cand", k)[:], in_=src, func=ACT.Tanh)
+
+        def keep_term(k):
+            gr, j = divmod(k, CH_TILES)
+            g, jj = divmod(j, K_PASS // P)
+            nc.vector.tensor_tensor(
+                out=fresh("zh", k)[:].rearrange("p (t c) -> p t c", t=NODE_TILES),
+                in0=live["zg", k][:].rearrange("p (t c) -> p t c", t=NODE_TILES),
+                in1=h_sb[gr, g][:, :, jj * P : (jj + 1) * P],
+                op=ALU.mult,
+            )
+
+        def new_term(k):
+            nc.vector.scalar_tensor_tensor(
+                out=fresh("zc", k)[:], in0=live["zg", k][:], scalar=1.0, in1=live["cand", k][:],
+                op0=ALU.subtract, op1=ALU.mult,
+            )
+
+        def finish(k):
+            gr, j = divmod(k, CH_TILES)
+            res = work.tile([P, NODES], F32, tag="res", bufs=4, name="res")
+            nc.vector.tensor_tensor(out=res[:], in0=live["zh", k][:], in1=live["zc", k][:], op=ALU.subtract)
+            dst = out[gr].rearrange("(t p) c -> p t c", p=P)[:, :, j * P : (j + 1) * P]
+            nc.sync.dma_start(out=dst, in_=res[:].rearrange("p (t c) -> p t c", t=NODE_TILES))
+
+        first = [(0, g, half) for g in range(PASSES) for half in range(2)]
+        for piece, (tag, bufs) in zip(first, (("ht", 1), ("fh", 1), ("fz", 2), ("fz", 2))):
+            h_transpose(piece, tag, bufs)
+            h_copy(piece)
+            h_quantize(piece)
+        bias_bank = psum.tile([P, P], BF16, tag="xt", name="bias_bank")
+        nc.tensor.transpose(bias_bank[:], bias_rows[:], ident_bf16[:])
+        nc.vector.tensor_copy(out=bias[:], in_=bias_bank[:, 0 : 3 * CH_TILES])
+
+        second = [(1, g, half) for g in range(PASSES) for half in range(2)]
+        second_from = 2
+
+        def at(fn, k):
+            if 0 <= k < UNITS:
+                fn(k)
+
+        for k in range(UNITS + 2):
+            at(cand_tanh, k - 2)
+            at(lambda i: recurrent(i, Z, "z"), k)
+            at(new_term, k - 2)
+            at(z_evacuate, k)
+            at(lambda i: recurrent(i, CAND, "c"), k - 1)
+            at(lambda i: recurrent(i, R, "r"), k)
+            if k == 0:
+                xr_turn(0)
+            at(xr_copy, k)
+            at(reset_product, k - 1)
+            at(z_sigmoid, k - 1)
+            at(r_add, k)
+            at(z_turn, k)
+            if 0 <= k - 1 - second_from < len(second):
+                h_copy(second[k - 1 - second_from])
+            at(r_sigmoid, k)
+            at(finish, k - 2)
+            at(keep_term, k - 1)
+            if 0 <= k - 1 - second_from < len(second):
+                h_quantize(second[k - 1 - second_from])
+            at(xr_turn, k + 1)
+            if 0 <= k - second_from < len(second):
+                h_transpose(second[k - second_from], "ht", 1)
+            at(cand_turn, k - 1)

@@ -17,13 +17,22 @@ P = 128
 GRAPHS = 2
 NODES = 512
 C = 1024
-PASSES = 2
 K_PASS = 512
+PASSES = C // K_PASS
 NODE_TILES = NODES // P
 CH_TILES = C // P
-CHUNK = 512
 UNITS = GRAPHS * CH_TILES
+LAST = UNITS - 1
 Z, R, CAND = 0, 1, 2
+BOUNDS = (0, 256, 512, 1024)
+CHUNKS = len(BOUNDS) - 1
+WHOLE = (0, NODE_TILES)
+HALVES = ((0, 2), (2, 4))
+SECOND_FROM = 2
+G_UNITS = 14
+Z_PE = 0
+H_PRE = 2
+Z_ALL_PE_FROM = 14
 FLOPS = 2 * GRAPHS * NODES * C * 3 * C
 
 
@@ -46,58 +55,68 @@ def tile_gatedgraphconvolution_pb_kernel(tc, x_proj, annotations, w_words, w_sca
                 h_sb[gr, g] = keep.tile([P, NODE_TILES, K_PASS], BF16, name="h_%d_%d" % (gr, g))
                 h_codes[gr, g] = keep.tile([P, NODES], U32, name="hc_%d_%d" % (gr, g), align_bytes=64)
                 h_scales[gr, g] = keep.tile([P, NODES], U8, name="hs_%d_%d" % (gr, g), align_bytes=64)
-        for gate in range(3):
-            for ck in range(C // CHUNK):
-                w_sb[gate, ck] = keep.tile([P, PASSES, 2 * CHUNK], U8, name="w_%d_%d" % (gate, ck), align_bytes=64)
+        for gate in (Z, R, CAND):
+            for ck in range(CHUNKS):
+                width = BOUNDS[ck + 1] - BOUNDS[ck]
+                w_sb[gate, ck] = keep.tile([P, PASSES, 2 * width], U8, name="w_%d_%d" % (gate, ck), align_bytes=64)
                 for gr in range(GRAPHS):
-                    x_sb[gr, gate, ck] = keep.tile([P, NODE_TILES, CHUNK], BF16, name="x_%d_%d_%d" % (gr, gate, ck))
+                    x_sb[gr, gate, ck] = keep.tile([P, NODE_TILES, width], BF16, name="x_%d_%d_%d" % (gr, gate, ck))
 
         def load_h(gr, g, t0, t1):
             src = annotations[gr].rearrange("(t p) k -> p t k", p=P)
             nc.sync.dma_start(out=h_sb[gr, g][:, t0:t1, :], in_=src[:, t0:t1, g * K_PASS : (g + 1) * K_PASS])
 
         def load_w(gate, ck):
-            c0 = 2 * (gate * C + ck * CHUNK)
-            src = w_words[:, :, c0 : c0 + 2 * CHUNK].rearrange("g p b -> p g b")
-            nc.sync.dma_start(out=w_sb[gate, ck][:].bitcast(I32), in_=src.bitcast(I32))
+            src = w_words[:, :, 2 * (gate * C + BOUNDS[ck]) : 2 * (gate * C + BOUNDS[ck + 1])]
+            nc.sync.dma_start(out=w_sb[gate, ck][:].bitcast(I32), in_=src.rearrange("g p b -> p g b").bitcast(I32))
 
         def load_x(gr, gate, ck):
-            c0 = gate * C + ck * CHUNK
-            src = x_proj[gr * NODES : (gr + 1) * NODES, c0 : c0 + CHUNK].rearrange("(t p) c -> p t c", p=P)
-            nc.sync.dma_start(out=x_sb[gr, gate, ck][:], in_=src)
+            src = x_proj[gr * NODES : (gr + 1) * NODES, gate * C + BOUNDS[ck] : gate * C + BOUNDS[ck + 1]]
+            nc.sync.dma_start(out=x_sb[gr, gate, ck][:], in_=src.rearrange("(t p) c -> p t c", p=P))
 
-        make_identity(nc, ident_f32[:])
-        nc.gpsimd.memset(bias_rows[:], 0.0)
+        warm_in = keep.tile([P, 1], F32, name="warm_in")
+        warm_out = keep.tile([P, 1], F32, name="warm_out")
+        nc.vector.memset(warm_in[:], 0.0)
+        nc.scalar.activation(out=warm_out[:], in_=warm_in[:], func=ACT.Sigmoid)
         make_identity(nc, ident_bf16[:])
+        make_identity(nc, ident_f32[:])
+        nc.vector.memset(bias_rows[:], 0.0)
         nc.scalar.dma_start(out=bias_rows[0 : 3 * CH_TILES, :], in_=bias_h.rearrange("(r c) -> r c", c=P))
 
-        for g in range(PASSES):
-            load_h(0, g, 0, 2)
-            load_h(0, g, 2, 4)
+        pieces = [[(gr, g, half) for g in range(PASSES) for half in range(2)] for gr in range(GRAPHS)]
+        for gr, g, half in pieces[0]:
+            load_h(gr, g, *HALVES[half])
+        load_x(0, R, 0)
         for q in range(4):
             nc.sync.dma_start(
                 out=scale_plane[32 * q : 32 * q + 4, :, :].bitcast(I32),
                 in_=w_scales[:, 4 * q : 4 * q + 4, :].rearrange("g r n -> r g n").bitcast(I32),
             )
-        load_w(Z, 0)
-        load_w(R, 0)
-        load_x(0, R, 0)
-        load_x(0, Z, 0)
-        load_w(CAND, 0)
-        load_x(0, CAND, 0)
-        for g in range(PASSES):
-            load_h(1, g, 0, 4)
-        for gate in (Z, R, CAND):
-            load_w(gate, 1)
-        for gr, ck in ((0, 1), (1, 0), (1, 1)):
+        for gate in (R, Z, CAND):
+            load_w(gate, 0)
+        for ck in range(1, CHUNKS):
+            load_x(0, CAND, ck - 1)
+            load_x(0, R, ck)
+            load_x(0, Z, ck - 1)
             for gate in (R, Z, CAND):
-                load_x(gr, gate, ck)
+                load_w(gate, ck)
+            if ck == 1:
+                for g in range(PASSES):
+                    load_h(1, g, *WHOLE)
+        for gate in (CAND, Z):
+            load_x(0, gate, CHUNKS - 1)
+        for ck in range(CHUNKS):
+            for gate in (R, CAND, Z):
+                load_x(1, gate, ck)
 
         live = {}
 
-        def h_transpose(piece, tag, bufs):
+        def bank_tile(role, shape, dtype):
+            return psum.tile(shape, dtype, tag=role, name=role, bufs=2 if role == "xt" else 1)
+
+        def h_transpose(piece, role):
             gr, g, half = piece
-            bank = psum.tile([P, 2, 2, P], F32, tag=tag, bufs=bufs, name="ht_bank")
+            bank = bank_tile(role, [P, 2, 2, P], F32)
             for a in range(2):
                 words = h_sb[gr, g][:, 2 * half + a, :].bitcast(F32)
                 for u in range(2):
@@ -107,8 +126,8 @@ def tile_gatedgraphconvolution_pb_kernel(tc, x_proj, annotations, w_words, w_sca
         def h_copy(piece):
             grouped = work.tile([P, 2 * P * 4], BF16, name="grouped", align_bytes=64)
             nc.scalar.copy(
-                out=grouped[:].bitcast(F32).rearrange("p (a r u) -> p a r u", a=2, u=2),
-                in_=live["ht", piece][:].rearrange("p a u r -> p a r u"),
+                out=grouped[:].bitcast(F32).rearrange("p (a n u) -> p a n u", a=2, u=2),
+                in_=live["ht", piece][:].rearrange("p a u n -> p a n u"),
             )
             live["grouped", piece] = grouped
 
@@ -121,153 +140,219 @@ def tile_gatedgraphconvolution_pb_kernel(tc, x_proj, annotations, w_words, w_sca
                 in_=live["grouped", piece][:],
             )
 
-        def x_view(k, gate):
-            gr, j = divmod(k, CH_TILES)
-            ck, jj = divmod(j, CHUNK // P)
-            return x_sb[gr, gate, ck][:, :, jj * P : (jj + 1) * P]
+        def by_tile(ap):
+            return ap.rearrange("p (t c) -> p t c", c=P)
+
+        def chunk_of(k):
+            j = k % CH_TILES
+            ck = max(i for i in range(CHUNKS) if BOUNDS[i] <= j * P)
+            return ck, j * P - BOUNDS[ck]
+
+        def x_view(k, gate, t0, t1):
+            ck, c0 = chunk_of(k)
+            return x_sb[k // CH_TILES, gate, ck][:, t0:t1, c0 : c0 + P]
 
         def bias_col(k, gate):
             col = gate * CH_TILES + k % CH_TILES
             return bias[:, col : col + 1]
 
-        def recurrent(k, gate, tag):
+        def sbuf(name, k, t0, t1, dtype=F32, bufs=3):
+            if (name, k) not in live:
+                live[name, k] = work.tile([P, NODES], dtype, tag=name, name=name, bufs=bufs)
+            return live[name, k][:, t0 * P : t1 * P]
+
+        def bank_of(name, k, t0, t1):
+            first, bank = max((e for e in live[name, k] if e[0] <= t0), key=lambda e: e[0])
+            return bank[:, (t0 - first) * P : (t1 - first) * P]
+
+        def open_bank(name, k, t0, t1, role, dtype=F32):
+            bank = bank_tile(role, [P, (t1 - t0) * P], dtype)
+            live.setdefault((name, k), []).append((t0, bank))
+
+        def recurrent(k, gate):
             gr, j = divmod(k, CH_TILES)
-            ck, jj = divmod(j, CHUNK // P)
-            bank = psum.tile([P, NODES], F32, tag=tag, name="mx_bank")
-            c0 = gate * C + j * P
+            ck, c0 = chunk_of(k)
+            name = "zrc"[gate : gate + 1]
+            open_bank(name, k, *WHOLE, name)
             for g in range(PASSES):
                 nc.tensor.matmul_mx(
-                    out=bank[:],
-                    lhsT=w_sb[gate, ck][:, g, 2 * jj * P : 2 * (jj + 1) * P].bitcast(E2M1X4),
-                    lhsT_scale=scale_plane[:, g, c0 : c0 + P],
+                    out=bank_of(name, k, *WHOLE),
+                    lhsT=w_sb[gate, ck][:, g, 2 * c0 : 2 * (c0 + P)].bitcast(E2M1X4),
+                    lhsT_scale=scale_plane[:, g, gate * C + j * P : gate * C + (j + 1) * P],
                     rhs=h_codes[gr, g][:].bitcast(E5M2X4),
                     rhs_scale=h_scales[gr, g][:],
                     start=(g == 0),
                     stop=(g == PASSES - 1),
                 )
-            live[tag, k] = bank
 
-        def fresh(name, k, dtype=F32):
-            t = work.tile([P, NODES], dtype, tag=name, name=name)
-            live[name, k] = t
-            return t
+        def add_x(k, name, gate, t0, t1, start, stop):
+            nc.tensor.matmul(
+                out=by_tile(bank_of(name, k, t0, t1)), lhsT=ident_bf16[:], rhs=x_view(k, gate, t0, t1), start=start, stop=stop
+            )
 
-        def z_evacuate(k):
-            nc.scalar.activation(out=fresh("mz", k)[:], in_=live["z", k][:], func=ACT.Identity, bias=bias_col(k, Z))
-
-        def z_turn(k):
-            bank = psum.tile([P, NODE_TILES, P], F32, tag="fz", bufs=2, name="fz_bank")
-            mz = live["mz", k]
-            nc.tensor.matmul(out=bank[:], lhsT=ident_bf16[:], rhs=x_view(k, Z), start=True, stop=False)
-            for t in range(NODE_TILES):
+        def turn(k, src, name, t0, t1, start, stop):
+            for t in range(t0, t1):
                 nc.tensor.matmul(
-                    out=bank[:, t, :], lhsT=mz[:, t * P : (t + 1) * P], rhs=ident_f32[:],
-                    start=False, stop=(t == NODE_TILES - 1), is_transpose=True,
+                    out=bank_of(name, k, t, t + 1), lhsT=sbuf(src, k, t, t + 1), rhs=ident_f32[:],
+                    start=(start and t == t0), stop=(stop and t == t1 - 1), is_transpose=True,
                 )
-            live["fz", k] = bank
 
-        def z_sigmoid(k):
-            src = live["fz", k][:].rearrange("p t c -> p (t c)")
-            nc.scalar.activation(out=fresh("zg", k)[:], in_=src, func=ACT.Sigmoid)
+        def z_on_pe(k):
+            return NODE_TILES if k >= Z_ALL_PE_FROM else Z_PE
 
         def xr_turn(k):
-            bank = psum.tile([P, NODES], BF16, tag="xt", name="xt_bank")
-            xr = x_view(k, R)
+            open_bank("xt", k, *WHOLE, "xt", BF16)
             for t in range(NODE_TILES):
-                nc.tensor.transpose(bank[:, t * P : (t + 1) * P], xr[:, t, :], ident_bf16[:])
-            live["xt", k] = bank
+                nc.tensor.transpose(bank_of("xt", k, t, t + 1), x_view(k, R, t, t + 1)[:, 0, :], ident_bf16[:])
 
         def xr_copy(k):
-            nc.scalar.copy(out=fresh("xrt", k, BF16)[:], in_=live["xt", k][:])
+            nc.scalar.copy(out=sbuf("xrt", k, *WHOLE, BF16), in_=bank_of("xt", k, *WHOLE))
 
         def r_add(k):
-            nc.vector.tensor_tensor(out=fresh("ar", k)[:], in0=live["r", k][:], in1=live["xrt", k][:], op=ALU.add)
+            nc.vector.tensor_tensor(
+                out=sbuf("ar", k, *WHOLE), in0=bank_of("r", k, *WHOLE), in1=sbuf("xrt", k, *WHOLE), op=ALU.add
+            )
 
         def r_sigmoid(k):
-            nc.scalar.activation(out=fresh("rg", k)[:], in_=live["ar", k][:], func=ACT.Sigmoid, bias=bias_col(k, R))
+            nc.scalar.activation(out=sbuf("rg", k, *WHOLE), in_=sbuf("ar", k, *WHOLE), func=ACT.Sigmoid, bias=bias_col(k, R))
 
-        def reset_product(k):
+        def reset_product(k, t0, t1):
             nc.vector.scalar_tensor_tensor(
-                out=fresh("rc", k)[:], in0=live["c", k][:], scalar=bias_col(k, CAND), in1=live["rg", k][:],
-                op0=ALU.add, op1=ALU.mult,
+                out=sbuf("rc", k, t0, t1), in0=bank_of("c", k, t0, t1), scalar=bias_col(k, CAND),
+                in1=sbuf("rg", k, t0, t1), op0=ALU.add, op1=ALU.mult,
             )
 
-        def cand_turn(k):
-            bank = psum.tile([P, NODE_TILES, P], F32, tag="fh", bufs=1, name="fh_bank")
-            rc = live["rc", k]
-            for t in range(NODE_TILES):
-                nc.tensor.matmul(
-                    out=bank[:, t, :], lhsT=rc[:, t * P : (t + 1) * P], rhs=ident_f32[:],
-                    start=(t == 0), stop=False, is_transpose=True,
+        def cand_tanh(k, t0, t1):
+            nc.scalar.activation(out=sbuf("cand", k, t0, t1), in_=bank_of("fh", k, t0, t1), func=ACT.Tanh)
+
+        def z_evacuate(k, t0, t1):
+            nc.scalar.activation(
+                out=sbuf("mz", k, t0, t1), in_=bank_of("z", k, t0, t1), func=ACT.Identity, bias=bias_col(k, Z)
+            )
+
+        def z_add(k):
+            n = z_on_pe(k)
+            if n < NODE_TILES:
+                nc.vector.tensor_tensor(
+                    out=by_tile(sbuf("az", k, n, NODE_TILES)), in0=by_tile(bank_of("fz", k, n, NODE_TILES)),
+                    in1=x_view(k, Z, n, NODE_TILES), op=ALU.add,
                 )
-            nc.tensor.matmul(out=bank[:], lhsT=ident_bf16[:], rhs=x_view(k, CAND), start=False, stop=True)
-            live["fh", k] = bank
 
-        def cand_tanh(k):
-            src = live["fh", k][:].rearrange("p t c -> p (t c)")
-            nc.scalar.activation(out=fresh("cand", k)[:], in_=src, func=ACT.Tanh)
+        def z_sigmoid(k, t0, t1):
+            n = min(max(z_on_pe(k), t0), t1)
+            if n > t0:
+                nc.scalar.activation(out=sbuf("zg", k, t0, n), in_=bank_of("fz", k, t0, n), func=ACT.Sigmoid)
+            if n < t1:
+                nc.scalar.activation(out=sbuf("zg", k, n, t1), in_=sbuf("az", k, n, t1), func=ACT.Sigmoid)
 
-        def keep_term(k):
+        def keep_term(k, t0, t1):
             gr, j = divmod(k, CH_TILES)
-            g, jj = divmod(j, K_PASS // P)
-            nc.vector.tensor_tensor(
-                out=fresh("zh", k)[:].rearrange("p (t c) -> p t c", t=NODE_TILES),
-                in0=live["zg", k][:].rearrange("p (t c) -> p t c", t=NODE_TILES),
-                in1=h_sb[gr, g][:, :, jj * P : (jj + 1) * P],
-                op=ALU.mult,
+            g, c0 = divmod(j * P, K_PASS)
+            engine = nc.gpsimd if k < G_UNITS else nc.vector
+            engine.tensor_tensor(
+                out=by_tile(sbuf("zh", k, t0, t1, bufs=1)), in0=by_tile(sbuf("zg", k, t0, t1)),
+                in1=h_sb[gr, g][:, t0:t1, c0 : c0 + P], op=ALU.mult,
             )
 
-        def new_term(k):
+        def new_term(k, t0, t1):
             nc.vector.scalar_tensor_tensor(
-                out=fresh("zc", k)[:], in0=live["zg", k][:], scalar=1.0, in1=live["cand", k][:],
+                out=sbuf("zc", k, t0, t1), in0=sbuf("zg", k, t0, t1), scalar=1.0, in1=sbuf("cand", k, t0, t1),
                 op0=ALU.subtract, op1=ALU.mult,
             )
 
-        def finish(k):
+        def finish(k, t0, t1):
             gr, j = divmod(k, CH_TILES)
-            res = work.tile([P, NODES], F32, tag="res", bufs=4, name="res")
-            nc.vector.tensor_tensor(out=res[:], in0=live["zh", k][:], in1=live["zc", k][:], op=ALU.subtract)
-            dst = out[gr].rearrange("(t p) c -> p t c", p=P)[:, :, j * P : (j + 1) * P]
-            nc.sync.dma_start(out=dst, in_=res[:].rearrange("p (t c) -> p t c", t=NODE_TILES))
+            res = sbuf("res", k, t0, t1, bufs=4)
+            nc.vector.tensor_tensor(out=res, in0=sbuf("zh", k, t0, t1), in1=sbuf("zc", k, t0, t1), op=ALU.subtract)
+            dst = out[gr].rearrange("(t p) c -> p t c", p=P)[:, t0:t1, j * P : (j + 1) * P]
+            nc.sync.dma_start(out=dst, in_=by_tile(res))
 
-        first = [(0, g, half) for g in range(PASSES) for half in range(2)]
-        for piece, (tag, bufs) in zip(first, (("ht", 1), ("fh", 1), ("fz", 2), ("fz", 2))):
-            h_transpose(piece, tag, bufs)
+        warm_bank = bank_tile("c", [P, NODE_TILES, P], F32)
+        for i in range(3):
+            nc.tensor.matmul(
+                out=warm_bank[:], lhsT=ident_bf16[:], rhs=ident_bf16[:].unsqueeze(1).to_broadcast([P, NODE_TILES, P]),
+                start=True, stop=True,
+            )
+        for piece, role in zip(pieces[0], ("ht", "fh", "fz", "z")):
+            h_transpose(piece, role)
             h_copy(piece)
             h_quantize(piece)
-        bias_bank = psum.tile([P, P], BF16, tag="xt", name="bias_bank")
+        bias_bank = bank_tile("c", [P, P], BF16)
         nc.tensor.transpose(bias_bank[:], bias_rows[:], ident_bf16[:])
         nc.vector.tensor_copy(out=bias[:], in_=bias_bank[:, 0 : 3 * CH_TILES])
+        xr_turn(0)
+        xr_copy(0)
+        recurrent(0, R)
+        xr_turn(1)
+        r_add(0)
+        r_sigmoid(0)
+        xr_copy(1)
 
-        second = [(1, g, half) for g in range(PASSES) for half in range(2)]
-        second_from = 2
+        for k in range(LAST):
+            piece = k - SECOND_FROM
+            recurrent(k, Z)
+            if k >= 1:
+                z_add(k - 1)
+                cand_tanh(k - 1, *WHOLE)
+            recurrent(k, CAND)
+            z_evacuate(k, *WHOLE)
+            recurrent(k + 1, R)
+            reset_product(k, *WHOLE)
+            if k >= 1:
+                z_sigmoid(k - 1, *WHOLE)
+            open_bank("fz", k, *WHOLE, "fz")
+            open_bank("fh", k, *WHOLE, "fh")
+            if z_on_pe(k):
+                add_x(k, "fz", Z, 0, z_on_pe(k), True, False)
+            if H_PRE:
+                add_x(k, "fh", CAND, 0, H_PRE, True, False)
+            if k + 2 <= LAST:
+                xr_turn(k + 2)
+            turn(k, "mz", "fz", *WHOLE, not z_on_pe(k), True)
+            if 0 <= piece < 4:
+                h_transpose(pieces[1][piece], "ht")
+            turn(k, "rc", "fh", *WHOLE, not H_PRE, False)
+            add_x(k, "fh", CAND, H_PRE, NODE_TILES, False, True)
+            r_add(k + 1)
+            if k + 2 <= LAST:
+                xr_copy(k + 2)
+            r_sigmoid(k + 1)
+            if 0 <= piece < 4:
+                h_copy(pieces[1][piece])
+            if 1 <= piece <= 4:
+                h_quantize(pieces[1][piece - 1])
+            if k >= 2:
+                finish(k - 2, *WHOLE)
+            if k >= 1:
+                new_term(k - 1, *WHOLE)
+            if k >= 1:
+                keep_term(k - 1, *WHOLE)
 
-        def at(fn, k):
-            if 0 <= k < UNITS:
-                fn(k)
-
-        for k in range(UNITS + 2):
-            at(cand_tanh, k - 2)
-            at(lambda i: recurrent(i, Z, "z"), k)
-            at(new_term, k - 2)
-            at(z_evacuate, k)
-            at(lambda i: recurrent(i, CAND, "c"), k - 1)
-            at(lambda i: recurrent(i, R, "r"), k)
-            if k == 0:
-                xr_turn(0)
-            at(xr_copy, k)
-            at(reset_product, k - 1)
-            at(z_sigmoid, k - 1)
-            at(r_add, k)
-            at(z_turn, k)
-            if 0 <= k - 1 - second_from < len(second):
-                h_copy(second[k - 1 - second_from])
-            at(r_sigmoid, k)
-            at(finish, k - 2)
-            at(keep_term, k - 1)
-            if 0 <= k - 1 - second_from < len(second):
-                h_quantize(second[k - 1 - second_from])
-            at(xr_turn, k + 1)
-            if 0 <= k - second_from < len(second):
-                h_transpose(second[k - second_from], "ht", 1)
-            at(cand_turn, k - 1)
+        recurrent(LAST, CAND)
+        cand_tanh(LAST - 1, *WHOLE)
+        recurrent(LAST, Z)
+        z_sigmoid(LAST - 1, *WHOLE)
+        for half in HALVES:
+            reset_product(LAST, *half)
+        for half in HALVES:
+            z_evacuate(LAST, *half)
+        finish(LAST - 2, *WHOLE)
+        new_term(LAST - 1, *WHOLE)
+        keep_term(LAST - 1, *WHOLE)
+        for half, role in zip(HALVES, ("r", "ht")):
+            open_bank("fh", LAST, *half, role)
+            add_x(LAST, "fh", CAND, *half, True, False)
+            turn(LAST, "rc", "fh", *half, False, True)
+            cand_tanh(LAST, *half)
+        for half, role in zip(HALVES, ("xt", "fh")):
+            open_bank("fz", LAST, *half, role)
+            add_x(LAST, "fz", Z, *half, True, False)
+            turn(LAST, "mz", "fz", *half, False, True)
+            z_sigmoid(LAST, *half)
+        new_term(LAST, *HALVES[0])
+        finish(LAST - 1, *WHOLE)
+        keep_term(LAST, *HALVES[0])
+        new_term(LAST, *HALVES[1])
+        keep_term(LAST, *HALVES[1])
+        for half in HALVES:
+            finish(LAST, *half)

@@ -21,18 +21,19 @@ K_PASS = 512
 PASSES = C // K_PASS
 NODE_TILES = NODES // P
 CH_TILES = C // P
-UNITS = GRAPHS * CH_TILES
-LAST = UNITS - 1
+LAST = GRAPHS * CH_TILES - 1
 Z, R, CAND = 0, 1, 2
-BOUNDS = (0, 256, 512, 1024)
-CHUNKS = len(BOUNDS) - 1
+PRODUCT = ("hz", "hr", "hc")
 WHOLE = (0, NODE_TILES)
 HALVES = ((0, 2), (2, 4))
-SECOND_FROM = 2
-G_UNITS = 14
-Z_PE = 0
-H_PRE = 2
-Z_ALL_PE_FROM = 14
+
+BOUNDS = (0, 256, 512, 1024)
+CHUNKS = len(BOUNDS) - 1
+SECOND_GRAPH_FROM = 2
+Z_TILES_ON_PE = 3
+Z_VECTOR_UNITS = 2
+WARM_MATMULS = 3
+
 FLOPS = 2 * GRAPHS * NODES * C * 3 * C
 
 
@@ -48,19 +49,20 @@ def tile_gatedgraphconvolution_pb_kernel(tc, x_proj, annotations, w_words, w_sca
         ident_bf16 = keep.tile([P, P], BF16, name="ident_bf16")
         bias_rows = keep.tile([P, P], BF16, name="bias_rows")
         bias = keep.tile([P, 3 * CH_TILES], F32, name="bias")
-        scale_plane = keep.tile([P, PASSES, 3 * C], U8, name="scale_plane", align_bytes=64)
+        w_scale_sb = keep.tile([P, PASSES, 3 * C], U8, name="w_scale_sb", align_bytes=64)
         h_sb, h_codes, h_scales, w_sb, x_sb = {}, {}, {}, {}, {}
         for gr in range(GRAPHS):
             for g in range(PASSES):
                 h_sb[gr, g] = keep.tile([P, NODE_TILES, K_PASS], BF16, name="h_%d_%d" % (gr, g))
-                h_codes[gr, g] = keep.tile([P, NODES], U32, name="hc_%d_%d" % (gr, g), align_bytes=64)
-                h_scales[gr, g] = keep.tile([P, NODES], U8, name="hs_%d_%d" % (gr, g), align_bytes=64)
+                h_codes[gr, g] = keep.tile([P, NODES], U32, name="h_codes_%d_%d" % (gr, g), align_bytes=64)
+                h_scales[gr, g] = keep.tile([P, NODES], U8, name="h_scales_%d_%d" % (gr, g), align_bytes=64)
         for gate in (Z, R, CAND):
             for ck in range(CHUNKS):
                 width = BOUNDS[ck + 1] - BOUNDS[ck]
                 w_sb[gate, ck] = keep.tile([P, PASSES, 2 * width], U8, name="w_%d_%d" % (gate, ck), align_bytes=64)
                 for gr in range(GRAPHS):
                     x_sb[gr, gate, ck] = keep.tile([P, NODE_TILES, width], BF16, name="x_%d_%d_%d" % (gr, gate, ck))
+
 
         def load_h(gr, g, t0, t1):
             src = annotations[gr].rearrange("(t p) k -> p t k", p=P)
@@ -78,19 +80,20 @@ def tile_gatedgraphconvolution_pb_kernel(tc, x_proj, annotations, w_words, w_sca
         warm_out = keep.tile([P, 1], F32, name="warm_out")
         nc.vector.memset(warm_in[:], 0.0)
         nc.scalar.activation(out=warm_out[:], in_=warm_in[:], func=ACT.Sigmoid)
+
         make_identity(nc, ident_bf16[:])
         make_identity(nc, ident_f32[:])
         nc.vector.memset(bias_rows[:], 0.0)
         nc.scalar.dma_start(out=bias_rows[0 : 3 * CH_TILES, :], in_=bias_h.rearrange("(r c) -> r c", c=P))
 
-        pieces = [[(gr, g, half) for g in range(PASSES) for half in range(2)] for gr in range(GRAPHS)]
-        for gr, g, half in pieces[0]:
+        quarters = [[(gr, g, half) for g in range(PASSES) for half in range(2)] for gr in range(GRAPHS)]
+        for gr, g, half in quarters[0]:
             load_h(gr, g, *HALVES[half])
         load_x(0, R, 0)
-        for q in range(4):
+        for i in range(4):
             nc.sync.dma_start(
-                out=scale_plane[32 * q : 32 * q + 4, :, :].bitcast(I32),
-                in_=w_scales[:, 4 * q : 4 * q + 4, :].rearrange("g r n -> r g n").bitcast(I32),
+                out=w_scale_sb[i:P:32, :, :].bitcast(I32),
+                in_=w_scales[:, i:16:4, :].rearrange("g q n -> q g n").bitcast(I32),
             )
         for gate in (R, Z, CAND):
             load_w(gate, 0)
@@ -109,44 +112,32 @@ def tile_gatedgraphconvolution_pb_kernel(tc, x_proj, annotations, w_words, w_sca
             for gate in (R, CAND, Z):
                 load_x(1, gate, ck)
 
+
         live = {}
 
         def bank_tile(role, shape, dtype):
-            return psum.tile(shape, dtype, tag=role, name=role, bufs=2 if role == "xt" else 1)
+            return psum.tile(shape, dtype, tag=role, name=role, bufs=2 if role == "az" else 1)
 
-        def h_transpose(piece, role):
-            gr, g, half = piece
-            bank = bank_tile(role, [P, 2, 2, P], F32)
-            for a in range(2):
-                words = h_sb[gr, g][:, 2 * half + a, :].bitcast(F32)
-                for u in range(2):
-                    nc.tensor.transpose(bank[:, a, u, :], words[:, u : 2 * P : 2], ident_f32[:])
-            live["ht", piece] = bank
+        def open_bank(name, k, t0, t1, role, dtype=F32):
+            bank = bank_tile(role, [P, (t1 - t0) * P], dtype)
+            live.setdefault((name, k), []).append((t0, bank))
 
-        def h_copy(piece):
-            grouped = work.tile([P, 2 * P * 4], BF16, name="grouped", align_bytes=64)
-            nc.scalar.copy(
-                out=grouped[:].bitcast(F32).rearrange("p (a n u) -> p a n u", a=2, u=2),
-                in_=live["ht", piece][:].rearrange("p a u n -> p a n u"),
-            )
-            live["grouped", piece] = grouped
+        def bank_of(name, k, t0, t1):
+            first, bank = max((entry for entry in live[name, k] if entry[0] <= t0), key=lambda entry: entry[0])
+            return bank[:, (t0 - first) * P : (t1 - first) * P]
 
-        def h_quantize(piece):
-            gr, g, half = piece
-            cols = slice(half * 2 * P, (half + 1) * 2 * P)
-            nc.vector.quantize_mx(
-                out=h_codes[gr, g][:, cols].bitcast(E5M2X4),
-                scales=h_scales[gr, g][:, cols],
-                in_=live["grouped", piece][:],
-            )
+        def sbuf(name, k, t0, t1, dtype=F32, bufs=3):
+            if (name, k) not in live:
+                live[name, k] = work.tile([P, NODES], dtype, tag=name, name=name, bufs=bufs)
+            return live[name, k][:, t0 * P : t1 * P]
 
         def by_tile(ap):
             return ap.rearrange("p (t c) -> p t c", c=P)
 
         def chunk_of(k):
-            j = k % CH_TILES
-            ck = max(i for i in range(CHUNKS) if BOUNDS[i] <= j * P)
-            return ck, j * P - BOUNDS[ck]
+            c0 = k % CH_TILES * P
+            ck = max(i for i in range(CHUNKS) if BOUNDS[i] <= c0)
+            return ck, c0 - BOUNDS[ck]
 
         def x_view(k, gate, t0, t1):
             ck, c0 = chunk_of(k)
@@ -156,29 +147,43 @@ def tile_gatedgraphconvolution_pb_kernel(tc, x_proj, annotations, w_words, w_sca
             col = gate * CH_TILES + k % CH_TILES
             return bias[:, col : col + 1]
 
-        def sbuf(name, k, t0, t1, dtype=F32, bufs=3):
-            if (name, k) not in live:
-                live[name, k] = work.tile([P, NODES], dtype, tag=name, name=name, bufs=bufs)
-            return live[name, k][:, t0 * P : t1 * P]
 
-        def bank_of(name, k, t0, t1):
-            first, bank = max((e for e in live[name, k] if e[0] <= t0), key=lambda e: e[0])
-            return bank[:, (t0 - first) * P : (t1 - first) * P]
+        def h_transpose(quarter, role):
+            gr, g, half = quarter
+            bank = bank_tile(role, [P, 2, 2, P], F32)
+            for a in range(2):
+                words = h_sb[gr, g][:, 2 * half + a, :].bitcast(F32)
+                for u in range(2):
+                    nc.tensor.transpose(bank[:, a, u, :], words[:, u : 2 * P : 2], ident_f32[:])
+            live["h_words", quarter] = bank
 
-        def open_bank(name, k, t0, t1, role, dtype=F32):
-            bank = bank_tile(role, [P, (t1 - t0) * P], dtype)
-            live.setdefault((name, k), []).append((t0, bank))
+        def h_copy(quarter):
+            grouped = work.tile([P, 2 * P * 4], BF16, name="grouped", align_bytes=64)
+            nc.scalar.copy(
+                out=grouped[:].bitcast(F32).rearrange("p (a n u) -> p a n u", a=2, u=2),
+                in_=live["h_words", quarter][:].rearrange("p a u n -> p a n u"),
+            )
+            live["grouped", quarter] = grouped
+
+        def h_quantize(quarter):
+            gr, g, half = quarter
+            nodes = slice(half * 2 * P, (half + 1) * 2 * P)
+            nc.vector.quantize_mx(
+                out=h_codes[gr, g][:, nodes].bitcast(E5M2X4),
+                scales=h_scales[gr, g][:, nodes],
+                in_=live["grouped", quarter][:],
+            )
+
 
         def recurrent(k, gate):
             gr, j = divmod(k, CH_TILES)
             ck, c0 = chunk_of(k)
-            name = "zrc"[gate : gate + 1]
-            open_bank(name, k, *WHOLE, name)
+            open_bank(PRODUCT[gate], k, *WHOLE, PRODUCT[gate])
             for g in range(PASSES):
                 nc.tensor.matmul_mx(
-                    out=bank_of(name, k, *WHOLE),
+                    out=bank_of(PRODUCT[gate], k, *WHOLE),
                     lhsT=w_sb[gate, ck][:, g, 2 * c0 : 2 * (c0 + P)].bitcast(E2M1X4),
-                    lhsT_scale=scale_plane[:, g, gate * C + j * P : gate * C + (j + 1) * P],
+                    lhsT_scale=w_scale_sb[:, g, gate * C + j * P : gate * C + (j + 1) * P],
                     rhs=h_codes[gr, g][:].bitcast(E5M2X4),
                     rhs_scale=h_scales[gr, g][:],
                     start=(g == 0),
@@ -187,7 +192,8 @@ def tile_gatedgraphconvolution_pb_kernel(tc, x_proj, annotations, w_words, w_sca
 
         def add_x(k, name, gate, t0, t1, start, stop):
             nc.tensor.matmul(
-                out=by_tile(bank_of(name, k, t0, t1)), lhsT=ident_bf16[:], rhs=x_view(k, gate, t0, t1), start=start, stop=stop
+                out=by_tile(bank_of(name, k, t0, t1)), lhsT=ident_bf16[:], rhs=x_view(k, gate, t0, t1),
+                start=start, stop=stop,
             )
 
         def turn(k, src, name, t0, t1, start, stop):
@@ -197,87 +203,91 @@ def tile_gatedgraphconvolution_pb_kernel(tc, x_proj, annotations, w_words, w_sca
                     start=(start and t == t0), stop=(stop and t == t1 - 1), is_transpose=True,
                 )
 
-        def z_on_pe(k):
-            return NODE_TILES if k >= Z_ALL_PE_FROM else Z_PE
-
         def xr_turn(k):
-            open_bank("xt", k, *WHOLE, "xt", BF16)
+            open_bank("xr_t", k, *WHOLE, "xr_t", BF16)
             for t in range(NODE_TILES):
-                nc.tensor.transpose(bank_of("xt", k, t, t + 1), x_view(k, R, t, t + 1)[:, 0, :], ident_bf16[:])
+                nc.tensor.transpose(bank_of("xr_t", k, t, t + 1), x_view(k, R, t, t + 1)[:, 0, :], ident_bf16[:])
+
+        def z_tiles_on_pe(k):
+            if k < Z_VECTOR_UNITS:
+                return 0
+            return NODE_TILES if k >= LAST - 1 else Z_TILES_ON_PE
+
 
         def xr_copy(k):
-            nc.scalar.copy(out=sbuf("xrt", k, *WHOLE, BF16), in_=bank_of("xt", k, *WHOLE))
+            nc.scalar.copy(out=sbuf("xr_sb", k, *WHOLE, BF16), in_=bank_of("xr_t", k, *WHOLE))
 
         def r_add(k):
             nc.vector.tensor_tensor(
-                out=sbuf("ar", k, *WHOLE), in0=bank_of("r", k, *WHOLE), in1=sbuf("xrt", k, *WHOLE), op=ALU.add
+                out=sbuf("ar", k, *WHOLE), in0=bank_of("hr", k, *WHOLE), in1=sbuf("xr_sb", k, *WHOLE), op=ALU.add
             )
 
         def r_sigmoid(k):
-            nc.scalar.activation(out=sbuf("rg", k, *WHOLE), in_=sbuf("ar", k, *WHOLE), func=ACT.Sigmoid, bias=bias_col(k, R))
+            nc.scalar.activation(out=sbuf("r", k, *WHOLE), in_=sbuf("ar", k, *WHOLE), func=ACT.Sigmoid, bias=bias_col(k, R))
 
         def reset_product(k, t0, t1):
             nc.vector.scalar_tensor_tensor(
-                out=sbuf("rc", k, t0, t1), in0=bank_of("c", k, t0, t1), scalar=bias_col(k, CAND),
-                in1=sbuf("rg", k, t0, t1), op0=ALU.add, op1=ALU.mult,
+                out=sbuf("r_hc", k, t0, t1), in0=bank_of("hc", k, t0, t1), scalar=bias_col(k, CAND),
+                in1=sbuf("r", k, t0, t1), op0=ALU.add, op1=ALU.mult,
             )
 
         def cand_tanh(k, t0, t1):
-            nc.scalar.activation(out=sbuf("cand", k, t0, t1), in_=bank_of("fh", k, t0, t1), func=ACT.Tanh)
+            nc.scalar.activation(out=sbuf("cand", k, t0, t1), in_=bank_of("ac", k, t0, t1), func=ACT.Tanh)
 
-        def z_evacuate(k, t0, t1):
+        def hz_copy(k, t0, t1):
             nc.scalar.activation(
-                out=sbuf("mz", k, t0, t1), in_=bank_of("z", k, t0, t1), func=ACT.Identity, bias=bias_col(k, Z)
+                out=sbuf("hz_sb", k, t0, t1), in_=bank_of("hz", k, t0, t1), func=ACT.Identity, bias=bias_col(k, Z)
             )
 
         def z_add(k):
-            n = z_on_pe(k)
+            n = z_tiles_on_pe(k)
             if n < NODE_TILES:
                 nc.vector.tensor_tensor(
-                    out=by_tile(sbuf("az", k, n, NODE_TILES)), in0=by_tile(bank_of("fz", k, n, NODE_TILES)),
+                    out=by_tile(sbuf("az_sb", k, n, NODE_TILES)), in0=by_tile(bank_of("az", k, n, NODE_TILES)),
                     in1=x_view(k, Z, n, NODE_TILES), op=ALU.add,
                 )
 
         def z_sigmoid(k, t0, t1):
-            n = min(max(z_on_pe(k), t0), t1)
+            n = min(z_tiles_on_pe(k), t1)
             if n > t0:
-                nc.scalar.activation(out=sbuf("zg", k, t0, n), in_=bank_of("fz", k, t0, n), func=ACT.Sigmoid)
+                nc.scalar.activation(out=sbuf("z", k, t0, n), in_=bank_of("az", k, t0, n), func=ACT.Sigmoid)
             if n < t1:
-                nc.scalar.activation(out=sbuf("zg", k, n, t1), in_=sbuf("az", k, n, t1), func=ACT.Sigmoid)
+                nc.scalar.activation(out=sbuf("z", k, n, t1), in_=sbuf("az_sb", k, n, t1), func=ACT.Sigmoid)
 
         def keep_term(k, t0, t1):
             gr, j = divmod(k, CH_TILES)
             g, c0 = divmod(j * P, K_PASS)
-            engine = nc.gpsimd if k < G_UNITS else nc.vector
-            engine.tensor_tensor(
-                out=by_tile(sbuf("zh", k, t0, t1, bufs=1)), in0=by_tile(sbuf("zg", k, t0, t1)),
+            nc.vector.tensor_tensor(
+                out=by_tile(sbuf("z_h", k, t0, t1)), in0=by_tile(sbuf("z", k, t0, t1)),
                 in1=h_sb[gr, g][:, t0:t1, c0 : c0 + P], op=ALU.mult,
             )
 
         def new_term(k, t0, t1):
             nc.vector.scalar_tensor_tensor(
-                out=sbuf("zc", k, t0, t1), in0=sbuf("zg", k, t0, t1), scalar=1.0, in1=sbuf("cand", k, t0, t1),
+                out=sbuf("z_cand", k, t0, t1), in0=sbuf("z", k, t0, t1), scalar=1.0, in1=sbuf("cand", k, t0, t1),
                 op0=ALU.subtract, op1=ALU.mult,
             )
 
         def finish(k, t0, t1):
             gr, j = divmod(k, CH_TILES)
             res = sbuf("res", k, t0, t1, bufs=4)
-            nc.vector.tensor_tensor(out=res, in0=sbuf("zh", k, t0, t1), in1=sbuf("zc", k, t0, t1), op=ALU.subtract)
+            nc.vector.tensor_tensor(out=res, in0=sbuf("z_h", k, t0, t1), in1=sbuf("z_cand", k, t0, t1), op=ALU.subtract)
             dst = out[gr].rearrange("(t p) c -> p t c", p=P)[:, t0:t1, j * P : (j + 1) * P]
             nc.sync.dma_start(out=dst, in_=by_tile(res))
 
-        warm_bank = bank_tile("c", [P, NODE_TILES, P], F32)
-        for i in range(3):
+
+        warm_bank = bank_tile("hc", [P, NODE_TILES, P], F32)
+        for i in range(WARM_MATMULS):
             nc.tensor.matmul(
                 out=warm_bank[:], lhsT=ident_bf16[:], rhs=ident_bf16[:].unsqueeze(1).to_broadcast([P, NODE_TILES, P]),
                 start=True, stop=True,
             )
-        for piece, role in zip(pieces[0], ("ht", "fh", "fz", "z")):
-            h_transpose(piece, role)
-            h_copy(piece)
-            h_quantize(piece)
-        bias_bank = bank_tile("c", [P, P], BF16)
+
+        for quarter, role in zip(quarters[0], ("h_words", "ac", "az", "hz")):
+            h_transpose(quarter, role)
+            h_copy(quarter)
+            h_quantize(quarter)
+        bias_bank = bank_tile("hc", [P, P], BF16)
         nc.tensor.transpose(bias_bank[:], bias_rows[:], ident_bf16[:])
         nc.vector.tensor_copy(out=bias[:], in_=bias_bank[:, 0 : 3 * CH_TILES])
         xr_turn(0)
@@ -288,45 +298,50 @@ def tile_gatedgraphconvolution_pb_kernel(tc, x_proj, annotations, w_words, w_sca
         r_sigmoid(0)
         xr_copy(1)
 
+
         for k in range(LAST):
-            piece = k - SECOND_FROM
+            q = k - SECOND_GRAPH_FROM
             recurrent(k, Z)
             if k >= 1:
                 z_add(k - 1)
                 cand_tanh(k - 1, *WHOLE)
             recurrent(k, CAND)
-            z_evacuate(k, *WHOLE)
+            hz_copy(k, *WHOLE)
             recurrent(k + 1, R)
             reset_product(k, *WHOLE)
             if k >= 1:
                 z_sigmoid(k - 1, *WHOLE)
-            open_bank("fz", k, *WHOLE, "fz")
-            open_bank("fh", k, *WHOLE, "fh")
-            if z_on_pe(k):
-                add_x(k, "fz", Z, 0, z_on_pe(k), True, False)
-            if H_PRE:
-                add_x(k, "fh", CAND, 0, H_PRE, True, False)
+
+            open_bank("az", k, *WHOLE, "az")
+            open_bank("ac", k, *WHOLE, "ac")
+            z_pe = z_tiles_on_pe(k)
+            xh_first = 0 if z_pe else NODE_TILES // 2
+            if z_pe:
+                add_x(k, "az", Z, 0, z_pe, True, False)
+            else:
+                add_x(k, "ac", CAND, 0, xh_first, True, False)
             if k + 2 <= LAST:
                 xr_turn(k + 2)
-            turn(k, "mz", "fz", *WHOLE, not z_on_pe(k), True)
-            if 0 <= piece < 4:
-                h_transpose(pieces[1][piece], "ht")
-            turn(k, "rc", "fh", *WHOLE, not H_PRE, False)
-            add_x(k, "fh", CAND, H_PRE, NODE_TILES, False, True)
+            turn(k, "hz_sb", "az", *WHOLE, not z_pe, True)
+            if 0 <= q < 4:
+                h_transpose(quarters[1][q], "h_words")
+            turn(k, "r_hc", "ac", *WHOLE, not xh_first, False)
+            add_x(k, "ac", CAND, xh_first, NODE_TILES, False, True)
+
             r_add(k + 1)
             if k + 2 <= LAST:
                 xr_copy(k + 2)
             r_sigmoid(k + 1)
-            if 0 <= piece < 4:
-                h_copy(pieces[1][piece])
-            if 1 <= piece <= 4:
-                h_quantize(pieces[1][piece - 1])
+            if 0 <= q < 4:
+                h_copy(quarters[1][q])
+            if 1 <= q <= 4:
+                h_quantize(quarters[1][q - 1])
             if k >= 2:
                 finish(k - 2, *WHOLE)
             if k >= 1:
                 new_term(k - 1, *WHOLE)
-            if k >= 1:
                 keep_term(k - 1, *WHOLE)
+
 
         recurrent(LAST, CAND)
         cand_tanh(LAST - 1, *WHOLE)
@@ -335,19 +350,19 @@ def tile_gatedgraphconvolution_pb_kernel(tc, x_proj, annotations, w_words, w_sca
         for half in HALVES:
             reset_product(LAST, *half)
         for half in HALVES:
-            z_evacuate(LAST, *half)
+            hz_copy(LAST, *half)
         finish(LAST - 2, *WHOLE)
         new_term(LAST - 1, *WHOLE)
         keep_term(LAST - 1, *WHOLE)
-        for half, role in zip(HALVES, ("r", "ht")):
-            open_bank("fh", LAST, *half, role)
-            add_x(LAST, "fh", CAND, *half, True, False)
-            turn(LAST, "rc", "fh", *half, False, True)
+        for half, role in zip(HALVES, ("hr", "h_words")):
+            open_bank("ac", LAST, *half, role)
+            add_x(LAST, "ac", CAND, *half, True, False)
+            turn(LAST, "r_hc", "ac", *half, False, True)
             cand_tanh(LAST, *half)
-        for half, role in zip(HALVES, ("xt", "fh")):
-            open_bank("fz", LAST, *half, role)
-            add_x(LAST, "fz", Z, *half, True, False)
-            turn(LAST, "mz", "fz", *half, False, True)
+        for half, role in zip(HALVES, ("xr_t", "ac")):
+            open_bank("az", LAST, *half, role)
+            add_x(LAST, "az", Z, *half, True, False)
+            turn(LAST, "hz_sb", "az", *half, False, True)
             z_sigmoid(LAST, *half)
         new_term(LAST, *HALVES[0])
         finish(LAST - 1, *WHOLE)

from contextlib import ExitStack

import concourse.mybir as mybir
from concourse.masks import make_identity

F32 = mybir.dt.float32
BF16 = mybir.dt.bfloat16
I32 = mybir.dt.int32
U32 = mybir.dt.uint32
U8 = mybir.dt.uint8
E5M2X4 = mybir.dt.float8_e5m2_x4
E2M1X4 = mybir.dt.float4_e2m1fn_x4
ACT = mybir.ActivationFunctionType
ALU = mybir.AluOpType

P = 128
GRAPHS = 2
NODES = 512
C = 1024
K_PASS = 512
PASSES = C // K_PASS
NODE_TILES = NODES // P
CH_TILES = C // P
LAST = GRAPHS * CH_TILES - 1
Z, R, CAND = 0, 1, 2
PRODUCT = ("hz", "hr", "hc")
WHOLE = (0, NODE_TILES)
HALVES = ((0, 2), (2, 4))

BOUNDS = (0, 256, 512, 1024)
CHUNKS = len(BOUNDS) - 1
SECOND_GRAPH_FROM = 2
Z_TILES_ON_PE = 3
Z_VECTOR_UNITS = 2
WARM_MATMULS = 3

FLOPS = 2 * GRAPHS * NODES * C * 3 * C


def tile_gatedgraphconvolution_pb_kernel(tc, x_proj, annotations, w_words, w_scales, bias_h, out):
    nc = tc.nc
    with ExitStack() as ctx:
        keep = ctx.enter_context(tc.tile_pool(name="keep", bufs=1))
        work = ctx.enter_context(tc.tile_pool(name="work", bufs=3))
        psum = ctx.enter_context(tc.psum_pool(name="psum", bufs=1))
        ctx.enter_context(tc.manual_schedule())

        ident_f32 = keep.tile([P, P], F32, name="ident_f32")
        ident_bf16 = keep.tile([P, P], BF16, name="ident_bf16")
        bias_rows = keep.tile([P, P], BF16, name="bias_rows")
        bias = keep.tile([P, 3 * CH_TILES], F32, name="bias")
        w_scale_sb = keep.tile([P, PASSES, 3 * C], U8, name="w_scale_sb", align_bytes=64)
        h_sb, h_codes, h_scales, w_sb, x_sb = {}, {}, {}, {}, {}
        for gr in range(GRAPHS):
            for g in range(PASSES):
                h_sb[gr, g] = keep.tile([P, NODE_TILES, K_PASS], BF16, name="h_%d_%d" % (gr, g))
                h_codes[gr, g] = keep.tile([P, NODES], U32, name="h_codes_%d_%d" % (gr, g), align_bytes=64)
                h_scales[gr, g] = keep.tile([P, NODES], U8, name="h_scales_%d_%d" % (gr, g), align_bytes=64)
        for gate in (Z, R, CAND):
            for ck in range(CHUNKS):
                width = BOUNDS[ck + 1] - BOUNDS[ck]
                w_sb[gate, ck] = keep.tile([P, PASSES, 2 * width], U8, name="w_%d_%d" % (gate, ck), align_bytes=64)
                for gr in range(GRAPHS):
                    x_sb[gr, gate, ck] = keep.tile([P, NODE_TILES, width], BF16, name="x_%d_%d_%d" % (gr, gate, ck))


        def load_h(gr, g, t0, t1):
            src = annotations[gr].rearrange("(t p) k -> p t k", p=P)
            nc.sync.dma_start(out=h_sb[gr, g][:, t0:t1, :], in_=src[:, t0:t1, g * K_PASS : (g + 1) * K_PASS])

        def load_w(gate, ck):
            src = w_words[:, :, 2 * (gate * C + BOUNDS[ck]) : 2 * (gate * C + BOUNDS[ck + 1])]
            nc.sync.dma_start(out=w_sb[gate, ck][:].bitcast(I32), in_=src.rearrange("g p b -> p g b").bitcast(I32))

        def load_x(gr, gate, ck):
            src = x_proj[gr * NODES : (gr + 1) * NODES, gate * C + BOUNDS[ck] : gate * C + BOUNDS[ck + 1]]
            nc.sync.dma_start(out=x_sb[gr, gate, ck][:], in_=src.rearrange("(t p) c -> p t c", p=P))

        warm_in = keep.tile([P, 1], F32, name="warm_in")
        warm_out = keep.tile([P, 1], F32, name="warm_out")
        nc.vector.memset(warm_in[:], 0.0)
        nc.scalar.activation(out=warm_out[:], in_=warm_in[:], func=ACT.Sigmoid)

        make_identity(nc, ident_bf16[:])
        make_identity(nc, ident_f32[:])
        nc.vector.memset(bias_rows[:], 0.0)
        nc.scalar.dma_start(out=bias_rows[0 : 3 * CH_TILES, :], in_=bias_h.rearrange("(r c) -> r c", c=P))

        quarters = [[(gr, g, half) for g in range(PASSES) for half in range(2)] for gr in range(GRAPHS)]
        for gr, g, half in quarters[0]:
            load_h(gr, g, *HALVES[half])
        load_x(0, R, 0)
        for i in range(4):
            nc.sync.dma_start(
                out=w_scale_sb[i:P:32, :, :].bitcast(I32),
                in_=w_scales[:, i:16:4, :].rearrange("g q n -> q g n").bitcast(I32),
            )
        for gate in (R, Z, CAND):
            load_w(gate, 0)
        for ck in range(1, CHUNKS):
            load_x(0, CAND, ck - 1)
            load_x(0, R, ck)
            load_x(0, Z, ck - 1)
            for gate in (R, Z, CAND):
                load_w(gate, ck)
            if ck == 1:
                for g in range(PASSES):
                    load_h(1, g, *WHOLE)
        for gate in (CAND, Z):
            load_x(0, gate, CHUNKS - 1)
        for ck in range(CHUNKS):
            for gate in (R, CAND, Z):
                load_x(1, gate, ck)


        live = {}

        def bank_tile(role, shape, dtype):
            return psum.tile(shape, dtype, tag=role, name=role, bufs=2 if role == "az" else 1)

        def open_bank(name, k, t0, t1, role, dtype=F32):
            bank = bank_tile(role, [P, (t1 - t0) * P], dtype)
            live.setdefault((name, k), []).append((t0, bank))

        def bank_of(name, k, t0, t1):
            first, bank = max((entry for entry in live[name, k] if entry[0] <= t0), key=lambda entry: entry[0])
            return bank[:, (t0 - first) * P : (t1 - first) * P]

        def sbuf(name, k, t0, t1, dtype=F32, bufs=3):
            if (name, k) not in live:
                live[name, k] = work.tile([P, NODES], dtype, tag=name, name=name, bufs=bufs)
            return live[name, k][:, t0 * P : t1 * P]

        def by_tile(ap):
            return ap.rearrange("p (t c) -> p t c", c=P)

        def chunk_of(k):
            c0 = k % CH_TILES * P
            ck = max(i for i in range(CHUNKS) if BOUNDS[i] <= c0)
            return ck, c0 - BOUNDS[ck]

        def x_view(k, gate, t0, t1):
            ck, c0 = chunk_of(k)
            return x_sb[k // CH_TILES, gate, ck][:, t0:t1, c0 : c0 + P]

        def bias_col(k, gate):
            col = gate * CH_TILES + k % CH_TILES
            return bias[:, col : col + 1]


        def h_transpose(quarter, role):
            gr, g, half = quarter
            bank = bank_tile(role, [P, 2, 2, P], F32)
            for a in range(2):
                words = h_sb[gr, g][:, 2 * half + a, :].bitcast(F32)
                for u in range(2):
                    nc.tensor.transpose(bank[:, a, u, :], words[:, u : 2 * P : 2], ident_f32[:])
            live["h_words", quarter] = bank

        def h_copy(quarter):
            grouped = work.tile([P, 2 * P * 4], BF16, name="grouped", align_bytes=64)
            nc.scalar.copy(
                out=grouped[:].bitcast(F32).rearrange("p (a n u) -> p a n u", a=2, u=2),
                in_=live["h_words", quarter][:].rearrange("p a u n -> p a n u"),
            )
            live["grouped", quarter] = grouped

        def h_quantize(quarter):
            gr, g, half = quarter
            nodes = slice(half * 2 * P, (half + 1) * 2 * P)
            nc.vector.quantize_mx(
                out=h_codes[gr, g][:, nodes].bitcast(E5M2X4),
                scales=h_scales[gr, g][:, nodes],
                in_=live["grouped", quarter][:],
            )


        def recurrent(k, gate):
            gr, j = divmod(k, CH_TILES)
            ck, c0 = chunk_of(k)
            open_bank(PRODUCT[gate], k, *WHOLE, PRODUCT[gate])
            for g in range(PASSES):
                nc.tensor.matmul_mx(
                    out=bank_of(PRODUCT[gate], k, *WHOLE),
                    lhsT=w_sb[gate, ck][:, g, 2 * c0 : 2 * (c0 + P)].bitcast(E2M1X4),
                    lhsT_scale=w_scale_sb[:, g, gate * C + j * P : gate * C + (j + 1) * P],
                    rhs=h_codes[gr, g][:].bitcast(E5M2X4),
                    rhs_scale=h_scales[gr, g][:],
                    start=(g == 0),
                    stop=(g == PASSES - 1),
                )

        def add_x(k, name, gate, t0, t1, start, stop):
            nc.tensor.matmul(
                out=by_tile(bank_of(name, k, t0, t1)), lhsT=ident_bf16[:], rhs=x_view(k, gate, t0, t1),
                start=start, stop=stop,
            )

        def turn(k, src, name, t0, t1, start, stop):
            for t in range(t0, t1):
                nc.tensor.matmul(
                    out=bank_of(name, k, t, t + 1), lhsT=sbuf(src, k, t, t + 1), rhs=ident_f32[:],
                    start=(start and t == t0), stop=(stop and t == t1 - 1), is_transpose=True,
                )

        def xr_turn(k):
            open_bank("xr_t", k, *WHOLE, "xr_t", BF16)
            for t in range(NODE_TILES):
                nc.tensor.transpose(bank_of("xr_t", k, t, t + 1), x_view(k, R, t, t + 1)[:, 0, :], ident_bf16[:])

        def z_tiles_on_pe(k):
            if k < Z_VECTOR_UNITS:
                return 0
            return NODE_TILES if k >= LAST - 1 else Z_TILES_ON_PE


        def xr_copy(k):
            nc.scalar.copy(out=sbuf("xr_sb", k, *WHOLE, BF16), in_=bank_of("xr_t", k, *WHOLE))

        def r_add(k):
            nc.vector.tensor_tensor(
                out=sbuf("ar", k, *WHOLE), in0=bank_of("hr", k, *WHOLE), in1=sbuf("xr_sb", k, *WHOLE), op=ALU.add
            )

        def r_sigmoid(k):
            nc.scalar.activation(out=sbuf("r", k, *WHOLE), in_=sbuf("ar", k, *WHOLE), func=ACT.Sigmoid, bias=bias_col(k, R))

        def reset_product(k, t0, t1):
            nc.vector.scalar_tensor_tensor(
                out=sbuf("r_hc", k, t0, t1), in0=bank_of("hc", k, t0, t1), scalar=bias_col(k, CAND),
                in1=sbuf("r", k, t0, t1), op0=ALU.add, op1=ALU.mult,
            )

        def cand_tanh(k, t0, t1):
            nc.scalar.activation(out=sbuf("cand", k, t0, t1), in_=bank_of("ac", k, t0, t1), func=ACT.Tanh)

        def hz_copy(k, t0, t1):
            nc.scalar.activation(
                out=sbuf("hz_sb", k, t0, t1), in_=bank_of("hz", k, t0, t1), func=ACT.Identity, bias=bias_col(k, Z)
            )

        def z_add(k):
            n = z_tiles_on_pe(k)
            if n < NODE_TILES:
                nc.vector.tensor_tensor(
                    out=by_tile(sbuf("az_sb", k, n, NODE_TILES)), in0=by_tile(bank_of("az", k, n, NODE_TILES)),
                    in1=x_view(k, Z, n, NODE_TILES), op=ALU.add,
                )

        def z_sigmoid(k, t0, t1):
            n = min(z_tiles_on_pe(k), t1)
            if n > t0:
                nc.scalar.activation(out=sbuf("z", k, t0, n), in_=bank_of("az", k, t0, n), func=ACT.Sigmoid)
            if n < t1:
                nc.scalar.activation(out=sbuf("z", k, n, t1), in_=sbuf("az_sb", k, n, t1), func=ACT.Sigmoid)

        def keep_term(k, t0, t1):
            gr, j = divmod(k, CH_TILES)
            g, c0 = divmod(j * P, K_PASS)
            nc.vector.tensor_tensor(
                out=by_tile(sbuf("z_h", k, t0, t1)), in0=by_tile(sbuf("z", k, t0, t1)),
                in1=h_sb[gr, g][:, t0:t1, c0 : c0 + P], op=ALU.mult,
            )

        def new_term(k, t0, t1):
            nc.vector.scalar_tensor_tensor(
                out=sbuf("z_cand", k, t0, t1), in0=sbuf("z", k, t0, t1), scalar=1.0, in1=sbuf("cand", k, t0, t1),
                op0=ALU.subtract, op1=ALU.mult,
            )

        def finish(k, t0, t1):
            gr, j = divmod(k, CH_TILES)
            res = sbuf("res", k, t0, t1, bufs=4)
            nc.vector.tensor_tensor(out=res, in0=sbuf("z_h", k, t0, t1), in1=sbuf("z_cand", k, t0, t1), op=ALU.subtract)
            dst = out[gr].rearrange("(t p) c -> p t c", p=P)[:, t0:t1, j * P : (j + 1) * P]
            nc.sync.dma_start(out=dst, in_=by_tile(res))


        warm_bank = bank_tile("hc", [P, NODE_TILES, P], F32)
        for i in range(WARM_MATMULS):
            nc.tensor.matmul(
                out=warm_bank[:], lhsT=ident_bf16[:], rhs=ident_bf16[:].unsqueeze(1).to_broadcast([P, NODE_TILES, P]),
                start=True, stop=True,
            )

        for quarter, role in zip(quarters[0], ("h_words", "ac", "az", "hz")):
            h_transpose(quarter, role)
            h_copy(quarter)
            h_quantize(quarter)
        bias_bank = bank_tile("hc", [P, P], BF16)
        nc.tensor.transpose(bias_bank[:], bias_rows[:], ident_bf16[:])
        nc.vector.tensor_copy(out=bias[:], in_=bias_bank[:, 0 : 3 * CH_TILES])
        xr_turn(0)
        xr_copy(0)
        recurrent(0, R)
        xr_turn(1)
        r_add(0)
        r_sigmoid(0)
        xr_copy(1)


        for k in range(LAST):
            q = k - SECOND_GRAPH_FROM
            recurrent(k, Z)
            if k >= 1:
                z_add(k - 1)
                cand_tanh(k - 1, *WHOLE)
            recurrent(k, CAND)
            hz_copy(k, *WHOLE)
            recurrent(k + 1, R)
            reset_product(k, *WHOLE)
            if k >= 1:
                z_sigmoid(k - 1, *WHOLE)

            open_bank("az", k, *WHOLE, "az")
            open_bank("ac", k, *WHOLE, "ac")
            z_pe = z_tiles_on_pe(k)
            xh_first = 0 if z_pe else NODE_TILES // 2
            if z_pe:
                add_x(k, "az", Z, 0, z_pe, True, False)
            else:
                add_x(k, "ac", CAND, 0, xh_first, True, False)
            if k + 2 <= LAST:
                xr_turn(k + 2)
            turn(k, "hz_sb", "az", *WHOLE, not z_pe, True)
            if 0 <= q < 4:
                h_transpose(quarters[1][q], "h_words")
            turn(k, "r_hc", "ac", *WHOLE, not xh_first, False)
            add_x(k, "ac", CAND, xh_first, NODE_TILES, False, True)

            r_add(k + 1)
            if k + 2 <= LAST:
                xr_copy(k + 2)
            r_sigmoid(k + 1)
            if 0 <= q < 4:
                h_copy(quarters[1][q])
            if 1 <= q <= 4:
                h_quantize(quarters[1][q - 1])
            if k >= 2:
                finish(k - 2, *WHOLE)
            if k >= 1:
                new_term(k - 1, *WHOLE)
                keep_term(k - 1, *WHOLE)


        recurrent(LAST, CAND)
        cand_tanh(LAST - 1, *WHOLE)
        recurrent(LAST, Z)
        z_sigmoid(LAST - 1, *WHOLE)
        for half in HALVES:
            reset_product(LAST, *half)
        for half in HALVES:
            hz_copy(LAST, *half)
        finish(LAST - 2, *WHOLE)
        new_term(LAST - 1, *WHOLE)
        keep_term(LAST - 1, *WHOLE)
        for half, role in zip(HALVES, ("hr", "h_words")):
            open_bank("ac", LAST, *half, role)
            add_x(LAST, "ac", CAND, *half, True, False)
            turn(LAST, "r_hc", "ac", *half, False, True)
            cand_tanh(LAST, *half)
        for half, role in zip(HALVES, ("xr_t", "ac")):
            open_bank("az", LAST, *half, role)
            add_x(LAST, "az", Z, *half, True, False)
            turn(LAST, "hz_sb", "az", *half, False, True)
            z_sigmoid(LAST, *half)
        new_term(LAST, *HALVES[0])
        finish(LAST - 1, *WHOLE)
        keep_term(LAST, *HALVES[0])
        new_term(LAST, *HALVES[1])
        keep_term(LAST, *HALVES[1])
        for half in HALVES:
            finish(LAST, *half)
